import numpy as np
import ml_dtypes


def mxq(x, axis, fmt="e4m3"):
    dtype, down = {"e4m3": (ml_dtypes.float8_e4m3fn, 7), "e5m2": (ml_dtypes.float8_e5m2, 14)}[fmt]
    v = np.moveaxis(np.asarray(x, np.float32).astype(ml_dtypes.bfloat16).astype(np.float64), axis, -1)
    blocks = v.reshape(v.shape[:-1] + (-1, 32))
    amax = np.abs(blocks).max(-1, keepdims=True)
    byte = np.maximum(np.where(amax > 0, np.frexp(amax)[1] - 1 + 127, 0) - down, 1)
    scale = np.exp2(byte - 127.0)
    codes = (blocks / scale).astype(np.float32).astype(dtype).astype(np.float64)
    return np.moveaxis((codes * scale).reshape(v.shape), -1, axis)


WIDE = False


def mx_kscale(k):
    if not WIDE:
        return np.ones(k)
    levels = np.array([10, -10, 5, -5, 0])
    a = np.random.permutation(np.resize(levels, k // 512 * 4)).reshape(k // 512, 4)
    idx = np.arange(k)
    return np.exp2(a[idx // 512, idx % 128 // 32])


BF16 = ml_dtypes.bfloat16


def bf(x):
    return np.asarray(x, np.float32).astype(BF16)


def f64(x):
    return np.asarray(x).astype(np.float64)


B, F, L, SEG, PRED, D, H = 16, 128, 48, 24, 192, 512, 256
R = B * F
T = PRED // SEG
EPS = 1e-15
MAXN = 1.0 - 1e-5


def norm(a):
    return np.sqrt(np.maximum(np.sum(a * a, axis=-1, keepdims=True), EPS))


def artanh(r):
    c = np.clip(r, -1.0 + 1e-7, 1.0 - 1e-7)
    return 0.5 * np.log((1.0 + c) / (1.0 - c))


def projx(a):
    n = norm(a)
    return np.where(n > MAXN, a * (MAXN / n), a)


def mobius_add(x, y):
    x2 = np.sum(x * x, -1, keepdims=True)
    y2 = np.sum(y * y, -1, keepdims=True)
    xy = np.sum(x * y, -1, keepdims=True)
    num = (1.0 + 2.0 * xy + y2) * x + (1.0 - x2) * y
    den = 1.0 + 2.0 * xy + x2 * y2
    return num / np.maximum(den, EPS)


def lam(x):
    return 2.0 / np.maximum(1.0 - np.sum(x * x, -1, keepdims=True), EPS)


def expmap(x, v):
    n = norm(v)
    second = np.tanh(lam(x) * n / 2.0) * v / n
    return projx(mobius_add(x, second))


def logmap0(x):
    n = norm(x)
    return artanh(n) * x / n


def setup_inputs():
    s = mx_kscale(D)
    c = np.exp2(np.ceil(np.log2(np.sqrt(np.mean(s * s)))))
    return {"z0": bf(np.random.standard_normal((R, D)) * 0.46 / np.sqrt(D) * s / c),
            "v0t": bf(np.random.standard_normal((R, D)) * 0.79 / np.sqrt(D) * s / c),
            "step_sizes": bf(-1.5 + 0.1 * np.random.standard_normal(1)),
            "W1": bf(np.random.standard_normal((D, H)) * c / s[:, None]),
            "b1": bf(np.random.standard_normal(H) * 0.3)}


def reference(z0, v0t, step_sizes, W1, b1):
    step = 1.0 / (1.0 + np.exp(-f64(step_sizes)))
    t_vals = np.arange(1, T + 1) * 1.0
    v_all = step * t_vals[None, :, None] * f64(v0t)[:, None, :]
    z_fut = expmap(f64(z0)[:, None, :], v_all)
    tan = logmap0(z_fut)
    return np.maximum((mxq(tan, 2, "e4m3") @ mxq(f64(W1), 0, "e4m3")) + f64(b1), 0.0)

@@ -1,0 +1,311 @@
+import math
+from contextlib import ExitStack
+
+import concourse.mybir as mybir
+from concourse.masks import make_identity
+
+F32 = mybir.dt.float32
+BF16 = mybir.dt.bfloat16
+U32 = mybir.dt.uint32
+U8 = mybir.dt.uint8
+FP8X4 = mybir.dt.float8_e4m3fn_x4
+ACT = mybir.ActivationFunctionType
+ALU = mybir.AluOpType
+
+P = 128
+ROWS = 2048
+D = 512
+STEPS = 8
+H = 256
+ROW_TILES = ROWS // P
+HALF = STEPS // 2
+WORDS = D // 2
+H_TILES = H // P
+FIRST_TILES = 4
+
+EPS = 1e-15
+MAXN = 1.0 - 1e-5
+TINY = 1e-30
+
+FLOPS = 2 * ROWS * STEPS * D * H
+
+
+def tile_directnodecomphyperbolicforecaster_pb_t_kernel(tc, z0, v0t, step_sizes, W1, b1, out):
+    nc = tc.nc
+    z0_rows = z0.rearrange("(p i) d -> p i d", i=ROW_TILES)
+    v0_rows = v0t.rearrange("(p i) d -> p i d", i=ROW_TILES)
+    out_rows = out.rearrange("(p i) t h -> p i t h", i=ROW_TILES)
+
+    with ExitStack() as ctx:
+        consts = ctx.enter_context(tc.tile_pool(name="consts", bufs=1))
+        coef = ctx.enter_context(tc.tile_pool(name="coef", bufs=1))
+        unread = ctx.enter_context(tc.tile_pool(name="unread", bufs=4))
+        stream = ctx.enter_context(tc.tile_pool(name="stream", bufs=3))
+        psum_in = ctx.enter_context(tc.psum_pool(name="psum_in", bufs=3))
+        psum_mm = ctx.enter_context(tc.psum_pool(name="psum_mm", bufs=2))
+        psum_out = ctx.enter_context(tc.psum_pool(name="psum_out", bufs=3))
+
+        z0_sb = consts.tile([P, ROW_TILES, D], BF16)
+        v0_sb = consts.tile([P, ROW_TILES, D], BF16)
+        raw_step = consts.tile([P, 1], BF16)
+        w_raw = consts.tile([P, 4, H], BF16)
+        b_rows = consts.tile([P, P], BF16)
+        nc.vector.memset(b_rows[:], 0.0)
+        nc.sync.dma_start(out=raw_step[:], in_=step_sizes.partition_broadcast(P))
+        for first in range(0, ROW_TILES, FIRST_TILES):
+            tiles = slice(first, first + FIRST_TILES)
+            nc.sync.dma_start(out=z0_sb[:, tiles, :], in_=z0_rows[:, tiles, :])
+            nc.sync.dma_start(out=v0_sb[:, tiles, :], in_=v0_rows[:, tiles, :])
+            if first == 0:
+                for u in range(2):
+                    nc.sync.dma_start(
+                        out=w_raw[:, 2 * u : 2 * u + 2, :],
+                        in_=W1[WORDS * u : WORDS * (u + 1), :].rearrange("(q e) c -> q e c", e=2),
+                    )
+                nc.sync.dma_start(out=b_rows[0:H_TILES, :], in_=b1.rearrange("(c h) -> c h", c=H_TILES))
+
+        warm = consts.tile([P, 1], F32)
+        nc.vector.memset(warm[:], 1.0)
+        nc.scalar.activation(out=warm[:], in_=warm[:], func=ACT.Sqrt)
+
+        ident = consts.tile([P, P], F32)
+        make_identity(nc, ident[:])
+
+        step_number = consts.tile([P, STEPS], F32)
+        for t in range(STEPS):
+            nc.vector.memset(step_number[:, t : t + 1], float(t + 1))
+
+        w_grouped = consts.tile([P, H, 4], BF16, align_bytes=64)
+        w_codes = consts.tile([P, H], U32, align_bytes=64)
+        w_scales = consts.tile([P, H], U8, align_bytes=64)
+        nc.vector.tensor_copy(out=w_grouped[:], in_=w_raw[:].rearrange("p j c -> p c j"))
+
+        b_rows32 = consts.tile([P, P], F32)
+        b_col = consts.tile([P, H_TILES], F32)
+        nc.vector.tensor_copy(out=b_rows32[:], in_=b_rows[:])
+        b_turned = psum_in.tile([P, P], F32, tag="turned")
+        nc.tensor.transpose(out=b_turned[:], in_=b_rows32[:], identity=ident[:])
+        nc.vector.tensor_copy(out=b_col[:], in_=b_turned[:, 0:H_TILES])
+        nc.vector.quantize_mx(
+            out=w_codes[:].bitcast(FP8X4), scales=w_scales[:], in_=w_grouped[:].rearrange("p c j -> p (c j)")
+        )
+
+        x2 = coef.tile([P, ROW_TILES], F32)
+        vv = coef.tile([P, ROW_TILES], F32)
+        xv = coef.tile([P, ROW_TILES], F32)
+
+        def scalar_sum_of_squares(x, total):
+            squares = unread.tile([P, D], BF16)
+            nc.scalar.activation(out=squares[:], in_=x, func=ACT.Square, accum_out=total)
+
+        def vector_sum_of_products(x, y, total):
+            products = unread.tile([P, D], F32)
+            nc.vector.scalar_tensor_tensor(
+                out=products[:], in0=x, scalar=1.0, in1=y, op0=ALU.mult, op1=ALU.mult, accum_out=total
+            )
+
+        def row_sums(i):
+            z_i, v_i = z0_sb[:, i, :], v0_sb[:, i, :]
+            scalar_sum_of_squares(z_i, x2[:, i : i + 1])
+            vector_sum_of_products(z_i, v_i, xv[:, i : i + 1])
+            if i < ROW_TILES // 2:
+                vector_sum_of_products(v_i, v_i, vv[:, i : i + 1])
+            else:
+                scalar_sum_of_squares(v_i, vv[:, i : i + 1])
+
+        def row_tile(name):
+            return coef.tile([P, ROW_TILES], F32, name=name)
+
+        def grid_tile(name):
+            return coef.tile([P, ROW_TILES, STEPS], F32, name=name)
+
+        step = consts.tile([P, 1], F32)
+        step_t = consts.tile([P, STEPS], F32)
+        step_t_capped = consts.tile([P, STEPS], F32)
+        one_minus_x2 = row_tile("one_minus_x2")
+        half_lambda = row_tile("half_lambda")
+        vv_floor = row_tile("vv_floor")
+        root_vv = row_tile("root_vv")
+        newton_row = row_tile("newton_row")
+        inv_root_vv = row_tile("inv_root_vv")
+        norm_v = grid_tile("norm_v")
+        tanh_arg = grid_tile("tanh_arg")
+        tanh_val = grid_tile("tanh_val")
+        y_over_v = grid_tile("y_over_v")
+        xy = grid_tile("xy")
+        y2 = grid_tile("y2")
+        two_xy_y2 = grid_tile("two_xy_y2")
+        den = grid_tile("den")
+        inv_den = grid_tile("inv_den")
+        norm2_m = grid_tile("norm2_m")
+        norm_m = grid_tile("norm_m")
+        newton = grid_tile("newton")
+        inv_norm_m = grid_tile("inv_norm_m")
+        norm_z = grid_tile("norm_z")
+        one_plus = grid_tile("one_plus")
+        one_minus = grid_tile("one_minus")
+        log_ratio = grid_tile("log_ratio")
+        gain = grid_tile("gain")
+        gain_z = grid_tile("gain_z")
+        gain_v = grid_tile("gain_v")
+        alpha = grid_tile("alpha")
+        beta = grid_tile("beta")
+
+        def step_sizes_times_t():
+            nc.scalar.activation(out=step[:], in_=raw_step[:], func=ACT.Tanh, scale=0.5)
+            nc.vector.tensor_scalar(out=step[:], in0=step[:], scalar1=0.5, scalar2=0.5, op0=ALU.mult, op1=ALU.add)
+            nc.vector.tensor_scalar(out=step_t[:], in0=step_number[:], scalar1=step[:, 0:1], scalar2=None, op0=ALU.mult)
+            nc.vector.tensor_scalar(
+                out=step_t_capped[:], in0=step_t[:], scalar1=1.0 / math.sqrt(EPS), scalar2=None, op0=ALU.mult
+            )
+
+        def coefficients(first, count, with_step):
+            shape = [P, count, STEPS]
+            v = nc.vector
+
+            def rows(x):
+                return x[:, first : first + count]
+
+            def grid(x):
+                return x[:, first : first + count, :]
+
+            def over_steps(x):
+                return rows(x).unsqueeze(2).to_broadcast(shape)
+
+            def over_rows(x):
+                return x[:].unsqueeze(1).to_broadcast(shape)
+
+            v.tensor_scalar(out=rows(one_minus_x2), in0=rows(x2), scalar1=-1.0, scalar2=1.0, op0=ALU.mult, op1=ALU.add)
+            v.tensor_scalar_max(out=rows(half_lambda), in0=rows(one_minus_x2), scalar1=EPS)
+            v.reciprocal(out=rows(half_lambda), in_=rows(half_lambda))
+            v.tensor_scalar_max(out=rows(vv_floor), in0=rows(vv), scalar1=TINY)
+            nc.scalar.activation(out=rows(root_vv), in_=rows(vv_floor), func=ACT.Sqrt)
+            v.reciprocal(out=rows(newton_row), in_=rows(root_vv))
+            v.scalar_tensor_tensor(
+                out=rows(newton_row), in0=rows(vv_floor), scalar=0.5, in1=rows(newton_row), op0=ALU.mult, op1=ALU.mult
+            )
+            v.scalar_tensor_tensor(
+                out=rows(root_vv), in0=rows(root_vv), scalar=0.5, in1=rows(newton_row), op0=ALU.mult, op1=ALU.add
+            )
+            v.reciprocal(out=rows(inv_root_vv), in_=rows(root_vv))
+            if with_step:
+                step_sizes_times_t()
+            v.tensor_tensor(out=grid(norm_v), in0=over_steps(root_vv), in1=over_rows(step_t), op=ALU.mult)
+            v.scalar_tensor_tensor(
+                out=grid(tanh_arg), in0=grid(norm_v), scalar=math.sqrt(EPS), in1=over_steps(half_lambda),
+                op0=ALU.max, op1=ALU.mult,
+            )
+            nc.scalar.activation(out=grid(tanh_val), in_=grid(tanh_arg), func=ACT.Tanh)
+            v.tensor_tensor(out=grid(y_over_v), in0=over_steps(inv_root_vv), in1=over_rows(step_t_capped), op=ALU.min)
+            v.tensor_mul(out=grid(y_over_v), in0=grid(y_over_v), in1=grid(tanh_val))
+            v.tensor_tensor(out=grid(xy), in0=grid(y_over_v), in1=over_steps(xv), op=ALU.mult)
+            v.tensor_tensor(out=grid(y2), in0=grid(y_over_v), in1=over_steps(vv), op=ALU.mult)
+            v.tensor_mul(out=grid(y2), in0=grid(y2), in1=grid(y_over_v))
+            v.scalar_tensor_tensor(
+                out=grid(two_xy_y2), in0=grid(xy), scalar=2.0, in1=grid(y2), op0=ALU.mult, op1=ALU.add
+            )
+            v.tensor_tensor(out=grid(den), in0=grid(y2), in1=over_steps(x2), op=ALU.mult)
+            v.scalar_tensor_tensor(out=grid(den), in0=grid(xy), scalar=2.0, in1=grid(den), op0=ALU.mult, op1=ALU.add)
+            v.tensor_scalar(out=grid(den), in0=grid(den), scalar1=1.0, scalar2=EPS, op0=ALU.add, op1=ALU.max)
+            v.reciprocal(out=grid(inv_den), in_=grid(den))
+            v.tensor_tensor(out=grid(norm2_m), in0=grid(two_xy_y2), in1=over_steps(x2), op=ALU.add)
+            v.tensor_mul(out=grid(norm2_m), in0=grid(norm2_m), in1=grid(inv_den))
+            v.tensor_scalar_max(out=grid(norm2_m), in0=grid(norm2_m), scalar1=EPS)
+            nc.scalar.activation(out=grid(norm_m), in_=grid(norm2_m), func=ACT.Sqrt)
+            v.reciprocal(out=grid(newton), in_=grid(norm_m))
+            v.scalar_tensor_tensor(
+                out=grid(newton), in0=grid(norm2_m), scalar=0.5, in1=grid(newton), op0=ALU.mult, op1=ALU.mult
+            )
+            v.scalar_tensor_tensor(
+                out=grid(norm_m), in0=grid(norm_m), scalar=0.5, in1=grid(newton), op0=ALU.mult, op1=ALU.add
+            )
+            v.tensor_scalar_min(out=grid(norm_z), in0=grid(norm_m), scalar1=MAXN)
+            v.tensor_scalar(out=grid(one_minus), in0=grid(norm_z), scalar1=-1.0, scalar2=1.0, op0=ALU.mult, op1=ALU.add)
+            v.reciprocal(out=grid(one_minus), in_=grid(one_minus))
+            v.tensor_scalar_add(out=grid(one_plus), in0=grid(norm_z), scalar1=1.0)
+            v.tensor_mul(out=grid(one_plus), in0=grid(one_plus), in1=grid(one_minus))
+            nc.scalar.activation(out=grid(log_ratio), in_=grid(one_plus), func=ACT.Ln)
+            v.reciprocal(out=grid(inv_norm_m), in_=grid(norm_m))
+            v.tensor_mul(out=grid(gain), in0=grid(inv_norm_m), in1=grid(inv_den))
+            v.scalar_tensor_tensor(
+                out=grid(gain_z), in0=grid(two_xy_y2), scalar=1.0, in1=grid(gain), op0=ALU.add, op1=ALU.mult
+            )
+            v.tensor_mul(out=grid(gain_v), in0=grid(y_over_v), in1=grid(gain))
+            v.tensor_tensor(out=grid(gain_v), in0=grid(gain_v), in1=over_steps(one_minus_x2), op=ALU.mult)
+            v.scalar_tensor_tensor(
+                out=grid(alpha), in0=grid(log_ratio), scalar=0.5, in1=grid(gain_z), op0=ALU.mult, op1=ALU.mult
+            )
+            v.scalar_tensor_tensor(
+                out=grid(beta), in0=grid(log_ratio), scalar=0.5, in1=grid(gain_v), op0=ALU.mult, op1=ALU.mult
+            )
+
+        for i in range(FIRST_TILES):
+            row_sums(i)
+        coefficients(0, FIRST_TILES, True)
+        for i in range(FIRST_TILES, ROW_TILES):
+            row_sums(i)
+        coefficients(FIRST_TILES, ROW_TILES - FIRST_TILES, False)
+
+        for i in range(ROW_TILES):
+            for half in range(2):
+                scaled_z = []
+                for q in range(HALF):
+                    t = half * HALF + q
+                    scaled = stream.tile([P, D], F32, bufs=6)
+                    if q < HALF - 1:
+                        nc.vector.tensor_scalar(
+                            out=scaled[:], in0=z0_sb[:, i, :], scalar1=alpha[:, i, t : t + 1], scalar2=None, op0=ALU.mult
+                        )
+                    else:
+                        nc.scalar.activation(out=scaled[:], in_=z0_sb[:, i, :], func=ACT.Copy, scale=alpha[:, i, t : t + 1])
+                    scaled_z.append(scaled)
+                tan = stream.tile([P, HALF * D], BF16)
+                for q in range(HALF):
+                    t = half * HALF + q
+                    nc.vector.scalar_tensor_tensor(
+                        out=tan[:, q * D : (q + 1) * D], in0=v0_sb[:, i, :], scalar=beta[:, i, t : t + 1],
+                        in1=scaled_z[q][:], op0=ALU.mult, op1=ALU.add,
+                    )
+
+                tan_words = tan[:].bitcast(F32)
+                grouped = stream.tile([P, HALF * P * 4], BF16, align_bytes=64)
+                grouped_words = grouped[:].bitcast(F32).rearrange("p (c u) -> p c u", u=2)
+                for pair in range(HALF // 2):
+                    turned = psum_in.tile([P, 2, 2 * P], F32, tag="turned")
+                    for q in range(2):
+                        for u in range(2):
+                            first_word = (2 * pair + q) * WORDS + u * P
+                            nc.tensor.transpose(
+                                out=turned[:, u, q * P : (q + 1) * P],
+                                in_=tan_words[:, first_word : first_word + P],
+                                identity=ident[:],
+                            )
+                    nc.scalar.copy(
+                        out=grouped_words[:, pair * 2 * P : (pair + 1) * 2 * P, :],
+                        in_=turned[:].rearrange("p u c -> p c u"),
+                    )
+
+                codes = stream.tile([P, HALF * P], U32, align_bytes=64)
+                scales = stream.tile([P, HALF * P], U8, align_bytes=64)
+                nc.vector.quantize_mx(out=codes[:].bitcast(FP8X4), scales=scales[:], in_=grouped[:])
+
+                result = stream.tile([P, HALF, H], F32)
+                for c in range(H_TILES):
+                    units = slice(c * P, (c + 1) * P)
+                    acc = psum_mm.tile([P, HALF * P], F32)
+                    nc.tensor.matmul_mx(
+                        out=acc[:],
+                        lhsT=w_codes[:, units].bitcast(FP8X4),
+                        lhsT_scale=w_scales[:, units],
+                        rhs=codes[:].bitcast(FP8X4),
+                        rhs_scale=scales[:],
+                        start=True,
+                        stop=True,
+                    )
+                    hidden = stream.tile([P, HALF * P], F32, bufs=4)
+                    nc.scalar.activation(out=hidden[:], in_=acc[:], func=ACT.Relu, bias=b_col[:, c : c + 1], scale=1.0)
+                    back = psum_out.tile([P, HALF, P], F32)
+                    for q in range(HALF):
+                        nc.tensor.transpose(out=back[:, q, :], in_=hidden[:, q * P : (q + 1) * P], identity=ident[:])
+                    nc.scalar.copy(out=result[:, :, units], in_=back[:])
+                nc.sync.dma_start(out=out_rows[:, i, half * HALF : (half + 1) * HALF, :], in_=result[:])

@@ -41,9 +41,10 @@ def tile_directnodecomphyperbolicforecaster_pb_t_kernel(tc, z0, v0t, step_sizes,
         coef = ctx.enter_context(tc.tile_pool(name="coef", bufs=1))
         unread = ctx.enter_context(tc.tile_pool(name="unread", bufs=4))
         stream = ctx.enter_context(tc.tile_pool(name="stream", bufs=3))
-        psum_in = ctx.enter_context(tc.psum_pool(name="psum_in", bufs=3))
+        psum_v0 = ctx.enter_context(tc.psum_pool(name="psum_v0", bufs=2))
+        psum_in = ctx.enter_context(tc.psum_pool(name="psum_in", bufs=2))
         psum_mm = ctx.enter_context(tc.psum_pool(name="psum_mm", bufs=2))
-        psum_out = ctx.enter_context(tc.psum_pool(name="psum_out", bufs=3))
+        psum_out = ctx.enter_context(tc.psum_pool(name="psum_out", bufs=2))
 
         z0_sb = consts.tile([P, ROW_TILES, D], BF16)
         v0_sb = consts.tile([P, ROW_TILES, D], BF16)
@@ -70,6 +71,8 @@ def tile_directnodecomphyperbolicforecaster_pb_t_kernel(tc, z0, v0t, step_sizes,
 
         ident = consts.tile([P, P], F32)
         make_identity(nc, ident[:])
+        ident_bf16 = consts.tile([P, P], BF16)
+        make_identity(nc, ident_bf16[:])
 
         step_number = consts.tile([P, STEPS], F32)
         for t in range(STEPS):
@@ -247,23 +250,23 @@ def tile_directnodecomphyperbolicforecaster_pb_t_kernel(tc, z0, v0t, step_sizes,
         coefficients(FIRST_TILES, ROW_TILES - FIRST_TILES, False)
 
         for i in range(ROW_TILES):
+            v0_psum = psum_v0.tile([P, D], F32)
+            nc.tensor.matmul(out=v0_psum[:], lhsT=ident_bf16[:], rhs=v0_sb[:, i, :], start=True, stop=True)
             for half in range(2):
                 scaled_z = []
                 for q in range(HALF):
                     t = half * HALF + q
-                    scaled = stream.tile([P, D], F32, bufs=6)
-                    if q < HALF - 1:
-                        nc.vector.tensor_scalar(
-                            out=scaled[:], in0=z0_sb[:, i, :], scalar1=alpha[:, i, t : t + 1], scalar2=None, op0=ALU.mult
-                        )
-                    else:
-                        nc.scalar.activation(out=scaled[:], in_=z0_sb[:, i, :], func=ACT.Copy, scale=alpha[:, i, t : t + 1])
+                    scaled = stream.tile([P, D], F32, bufs=8)
+                    nc.gpsimd.tensor_scalar(
+                        out=scaled[:], in0=z0_sb[:, i, :], scalar1=alpha[:, i, t : t + 1], scalar2=0.0,
+                        op0=ALU.mult, op1=ALU.add,
+                    )
                     scaled_z.append(scaled)
                 tan = stream.tile([P, HALF * D], BF16)
                 for q in range(HALF):
                     t = half * HALF + q
                     nc.vector.scalar_tensor_tensor(
-                        out=tan[:, q * D : (q + 1) * D], in0=v0_sb[:, i, :], scalar=beta[:, i, t : t + 1],
+                        out=tan[:, q * D : (q + 1) * D], in0=v0_psum[:], scalar=beta[:, i, t : t + 1],
                         in1=scaled_z[q][:], op0=ALU.mult, op1=ALU.add,
                     )
 

@@ -154,6 +154,9 @@ def tile_directnodecomphyperbolicforecaster_pb_t_kernel(tc, z0, v0t, step_sizes,
         alpha = grid_tile("alpha")
         beta = grid_tile("beta")
 
+        def load_table_of(func, after):
+            nc.scalar.activation(out=warm[:], in_=after, func=func)
+
         def step_sizes_times_t():
             nc.scalar.activation(out=step[:], in_=raw_step[:], func=ACT.Tanh, scale=0.5)
             nc.vector.tensor_scalar(out=step[:], in0=step[:], scalar1=0.5, scalar2=0.5, op0=ALU.mult, op1=ALU.add)
@@ -183,6 +186,7 @@ def tile_directnodecomphyperbolicforecaster_pb_t_kernel(tc, z0, v0t, step_sizes,
             v.reciprocal(out=rows(half_lambda), in_=rows(half_lambda))
             v.tensor_scalar_max(out=rows(vv_floor), in0=rows(vv), scalar1=TINY)
             nc.scalar.activation(out=rows(root_vv), in_=rows(vv_floor), func=ACT.Sqrt)
+            load_table_of(ACT.Tanh, root_vv[:, first : first + 1])
             v.reciprocal(out=rows(newton_row), in_=rows(root_vv))
             v.scalar_tensor_tensor(
                 out=rows(newton_row), in0=rows(vv_floor), scalar=0.5, in1=rows(newton_row), op0=ALU.mult, op1=ALU.mult
@@ -199,6 +203,7 @@ def tile_directnodecomphyperbolicforecaster_pb_t_kernel(tc, z0, v0t, step_sizes,
                 op0=ALU.max, op1=ALU.mult,
             )
             nc.scalar.activation(out=grid(tanh_val), in_=grid(tanh_arg), func=ACT.Tanh)
+            load_table_of(ACT.Sqrt, tanh_val[:, first, 0:1])
             v.tensor_tensor(out=grid(y_over_v), in0=over_steps(inv_root_vv), in1=over_rows(step_t_capped), op=ALU.min)
             v.tensor_mul(out=grid(y_over_v), in0=grid(y_over_v), in1=grid(tanh_val))
             v.tensor_tensor(out=grid(xy), in0=grid(y_over_v), in1=over_steps(xv), op=ALU.mult)
@@ -215,6 +220,7 @@ def tile_directnodecomphyperbolicforecaster_pb_t_kernel(tc, z0, v0t, step_sizes,
             v.tensor_mul(out=grid(norm2_m), in0=grid(norm2_m), in1=grid(inv_den))
             v.tensor_scalar_max(out=grid(norm2_m), in0=grid(norm2_m), scalar1=EPS)
             nc.scalar.activation(out=grid(norm_m), in_=grid(norm2_m), func=ACT.Sqrt)
+            load_table_of(ACT.Ln, norm2_m[:, first, 0:1])
             v.reciprocal(out=grid(newton), in_=grid(norm_m))
             v.scalar_tensor_tensor(
                 out=grid(newton), in0=grid(norm2_m), scalar=0.5, in1=grid(newton), op0=ALU.mult, op1=ALU.mult
@@ -228,6 +234,7 @@ def tile_directnodecomphyperbolicforecaster_pb_t_kernel(tc, z0, v0t, step_sizes,
             v.tensor_scalar_add(out=grid(one_plus), in0=grid(norm_z), scalar1=1.0)
             v.tensor_mul(out=grid(one_plus), in0=grid(one_plus), in1=grid(one_minus))
             nc.scalar.activation(out=grid(log_ratio), in_=grid(one_plus), func=ACT.Ln)
+            load_table_of(ACT.Sqrt, one_plus[:, first, 0:1])
             v.reciprocal(out=grid(inv_norm_m), in_=grid(norm_m))
             v.tensor_mul(out=grid(gain), in0=grid(inv_norm_m), in1=grid(inv_den))
             v.scalar_tensor_tensor(
@@ -310,5 +317,8 @@ def tile_directnodecomphyperbolicforecaster_pb_t_kernel(tc, z0, v0t, step_sizes,
                     back = psum_out.tile([P, HALF, P], F32)
                     for q in range(HALF):
                         nc.tensor.transpose(out=back[:, q, :], in_=hidden[:, q * P : (q + 1) * P], identity=ident[:])
-                    nc.scalar.copy(out=result[:, :, units], in_=back[:])
+                    if half == 1 and c == H_TILES - 1:
+                        nc.vector.tensor_copy(out=result[:, :, units], in_=back[:])
+                    else:
+                        nc.scalar.copy(out=result[:, :, units], in_=back[:])
                 nc.sync.dma_start(out=out_rows[:, i, half * HALF : (half + 1) * HALF, :], in_=result[:])

@@ -22,6 +22,9 @@ HALF = STEPS // 2
 WORDS = D // 2
 H_TILES = H // P
 FIRST_TILES = 4
+HALVES = 2 * ROW_TILES
+BANKS = 2 * HALVES
+MX_REPEATS = 2
 
 EPS = 1e-15
 MAXN = 1.0 - 1e-5
@@ -256,69 +259,117 @@ def tile_directnodecomphyperbolicforecaster_pb_t_kernel(tc, z0, v0t, step_sizes,
             row_sums(i)
         coefficients(FIRST_TILES, ROW_TILES - FIRST_TILES, False)
 
-        for i in range(ROW_TILES):
-            v0_psum = psum_v0.tile([P, D], F32)
-            nc.tensor.matmul(out=v0_psum[:], lhsT=ident_bf16[:], rhs=v0_sb[:, i, :], start=True, stop=True)
-            for half in range(2):
-                scaled_z = []
-                for q in range(HALF):
-                    t = half * HALF + q
-                    scaled = stream.tile([P, D], F32, bufs=8)
-                    nc.gpsimd.tensor_scalar(
-                        out=scaled[:], in0=z0_sb[:, i, :], scalar1=alpha[:, i, t : t + 1], scalar2=0.0,
-                        op0=ALU.mult, op1=ALU.add,
-                    )
-                    scaled_z.append(scaled)
-                tan = stream.tile([P, HALF * D], BF16)
-                for q in range(HALF):
-                    t = half * HALF + q
-                    nc.vector.scalar_tensor_tensor(
-                        out=tan[:, q * D : (q + 1) * D], in0=v0_psum[:], scalar=beta[:, i, t : t + 1],
-                        in1=scaled_z[q][:], op0=ALU.mult, op1=ALU.add,
+        scaled_z, v0_psum, tan, turned, grouped, codes, scales = {}, {}, {}, {}, {}, {}, {}
+        acc, hidden, back, result = {}, {}, {}, {}
+
+        def scale(s):
+            i = s // 2
+            scaled_z[s] = []
+            for q in range(HALF):
+                t = (s % 2) * HALF + q
+                scaled = stream.tile([P, D], F32, bufs=2 * HALF)
+                nc.gpsimd.tensor_scalar(
+                    out=scaled[:], in0=z0_sb[:, i, :], scalar1=alpha[:, i, t : t + 1], scalar2=0.0,
+                    op0=ALU.mult, op1=ALU.add,
+                )
+                scaled_z[s].append(scaled)
+
+        def copy_v0(i):
+            v0_psum[i] = psum_v0.tile([P, D], F32, name="v0_copy")
+            nc.tensor.matmul(out=v0_psum[i][:], lhsT=ident_bf16[:], rhs=v0_sb[:, i, :], start=True, stop=True)
+
+        def combine(s):
+            i = s // 2
+            tan[s] = stream.tile([P, HALF * D], BF16, name="tan")
+            for q in range(HALF):
+                t = (s % 2) * HALF + q
+                nc.vector.scalar_tensor_tensor(
+                    out=tan[s][:, q * D : (q + 1) * D], in0=v0_psum[i][:], scalar=beta[:, i, t : t + 1],
+                    in1=scaled_z[s][q][:], op0=ALU.mult, op1=ALU.add,
+                )
+
+        def turn_in(m):
+            s, pair = divmod(m, 2)
+            tan_words = tan[s][:].bitcast(F32)
+            turned[m] = psum_in.tile([P, 2, 2 * P], F32, name="turned", tag="turned")
+            for q in range(2):
+                for u in range(2):
+                    first_word = (2 * pair + q) * WORDS + u * P
+                    nc.tensor.transpose(
+                        out=turned[m][:, u, q * P : (q + 1) * P],
+                        in_=tan_words[:, first_word : first_word + P],
+                        identity=ident[:],
                     )
 
-                tan_words = tan[:].bitcast(F32)
-                grouped = stream.tile([P, HALF * P * 4], BF16, align_bytes=64)
-                grouped_words = grouped[:].bitcast(F32).rearrange("p (c u) -> p c u", u=2)
-                for pair in range(HALF // 2):
-                    turned = psum_in.tile([P, 2, 2 * P], F32, tag="turned")
-                    for q in range(2):
-                        for u in range(2):
-                            first_word = (2 * pair + q) * WORDS + u * P
-                            nc.tensor.transpose(
-                                out=turned[:, u, q * P : (q + 1) * P],
-                                in_=tan_words[:, first_word : first_word + P],
-                                identity=ident[:],
-                            )
-                    nc.scalar.copy(
-                        out=grouped_words[:, pair * 2 * P : (pair + 1) * 2 * P, :],
-                        in_=turned[:].rearrange("p u c -> p c u"),
-                    )
+        def gather(m):
+            s, pair = divmod(m, 2)
+            if pair == 0:
+                grouped[s] = stream.tile([P, HALF * P * 4], BF16, name="grouped", align_bytes=64)
+            grouped_words = grouped[s][:].bitcast(F32).rearrange("p (c u) -> p c u", u=2)
+            nc.scalar.copy(
+                out=grouped_words[:, pair * 2 * P : (pair + 1) * 2 * P, :],
+                in_=turned[m][:].rearrange("p u c -> p c u"),
+            )
 
-                codes = stream.tile([P, HALF * P], U32, align_bytes=64)
-                scales = stream.tile([P, HALF * P], U8, align_bytes=64)
-                nc.vector.quantize_mx(out=codes[:].bitcast(FP8X4), scales=scales[:], in_=grouped[:])
+        def quantise(s):
+            codes[s] = stream.tile([P, HALF * P], U32, name="codes", align_bytes=64)
+            scales[s] = stream.tile([P, HALF * P], U8, name="scales", align_bytes=64)
+            nc.vector.quantize_mx(out=codes[s][:].bitcast(FP8X4), scales=scales[s][:], in_=grouped[s][:])
 
-                result = stream.tile([P, HALF, H], F32)
-                for c in range(H_TILES):
-                    units = slice(c * P, (c + 1) * P)
-                    acc = psum_mm.tile([P, HALF * P], F32)
-                    nc.tensor.matmul_mx(
-                        out=acc[:],
-                        lhsT=w_codes[:, units].bitcast(FP8X4),
-                        lhsT_scale=w_scales[:, units],
-                        rhs=codes[:].bitcast(FP8X4),
-                        rhs_scale=scales[:],
-                        start=True,
-                        stop=True,
-                    )
-                    hidden = stream.tile([P, HALF * P], F32, bufs=4)
-                    nc.scalar.activation(out=hidden[:], in_=acc[:], func=ACT.Relu, bias=b_col[:, c : c + 1], scale=1.0)
-                    back = psum_out.tile([P, HALF, P], F32)
-                    for q in range(HALF):
-                        nc.tensor.transpose(out=back[:, q, :], in_=hidden[:, q * P : (q + 1) * P], identity=ident[:])
-                    if half == 1 and c == H_TILES - 1:
-                        nc.vector.tensor_copy(out=result[:, :, units], in_=back[:])
-                    else:
-                        nc.scalar.copy(out=result[:, :, units], in_=back[:])
-                nc.sync.dma_start(out=out_rows[:, i, half * HALF : (half + 1) * HALF, :], in_=result[:])
+        def multiply(m):
+            s, c = divmod(m, 2)
+            units = slice(c * P, (c + 1) * P)
+            acc[m] = psum_mm.tile([P, HALF * P], F32, name="acc")
+            for repeat in range(MX_REPEATS):
+                nc.tensor.matmul_mx(
+                    out=acc[m][:],
+                    lhsT=w_codes[:, units].bitcast(FP8X4),
+                    lhsT_scale=w_scales[:, units],
+                    rhs=codes[s][:].bitcast(FP8X4),
+                    rhs_scale=scales[s][:],
+                    start=True,
+                    stop=True,
+                )
+
+        def activate(m):
+            c = m % 2
+            hidden[m] = stream.tile([P, HALF * P], F32, name="hidden")
+            nc.scalar.activation(out=hidden[m][:], in_=acc[m][:], func=ACT.Relu, bias=b_col[:, c : c + 1], scale=1.0)
+
+        def turn_out(m):
+            back[m] = psum_out.tile([P, HALF, P], F32, name="back")
+            for q in range(HALF):
+                nc.tensor.transpose(out=back[m][:, q, :], in_=hidden[m][:, q * P : (q + 1) * P], identity=ident[:])
+
+        def collect(m):
+            s, c = divmod(m, 2)
+            units = slice(c * P, (c + 1) * P)
+            if c == 0:
+                result[s] = stream.tile([P, HALF, H], F32, name="result")
+            if m % 4 == 3:
+                nc.vector.tensor_copy(out=result[s][:, :, units], in_=back[m][:])
+            else:
+                nc.scalar.copy(out=result[s][:, :, units], in_=back[m][:])
+            if c == 1:
+                first_step = (s % 2) * HALF
+                nc.sync.dma_start(out=out_rows[:, s // 2, first_step : first_step + HALF, :], in_=result[s][:])
+
+        def if_any(stage, index, count):
+            if 0 <= index < count:
+                stage(index)
+
+        with tc.manual_schedule():
+            for m in range(-10, BANKS + 1):
+                if m % 2 == 0:
+                    n = m // 2
+                    if_any(scale, n + 5, HALVES)
+                    if (n + 5) % 2 == 0:
+                        if_any(copy_v0, (n + 5) // 2, ROW_TILES)
+                    if_any(quantise, n + 1, HALVES)
+                    if_any(combine, n + 4, HALVES)
+                if_any(turn_out, m - 1, BANKS)
+                if_any(turn_in, m + 5, BANKS)
+                if_any(multiply, m + 1, BANKS)
+                if_any(activate, m, BANKS)
+                if_any(gather, m + 4, BANKS)
+                if_any(collect, m - 1, BANKS)

import math
from contextlib import ExitStack

import concourse.mybir as mybir
from concourse.masks import make_identity

F32 = mybir.dt.float32
BF16 = mybir.dt.bfloat16
U32 = mybir.dt.uint32
U8 = mybir.dt.uint8
FP8X4 = mybir.dt.float8_e4m3fn_x4
ACT = mybir.ActivationFunctionType
ALU = mybir.AluOpType

P = 128
ROWS = 2048
D = 512
STEPS = 8
H = 256
ROW_TILES = ROWS // P
HALF = STEPS // 2
WORDS = D // 2
H_TILES = H // P
FIRST_TILES = 4
HALVES = 2 * ROW_TILES
BANKS = 2 * HALVES
MX_REPEATS = 2

EPS = 1e-15
MAXN = 1.0 - 1e-5
TINY = 1e-30

FLOPS = 2 * ROWS * STEPS * D * H


def tile_directnodecomphyperbolicforecaster_pb_t_kernel(tc, z0, v0t, step_sizes, W1, b1, out):
    nc = tc.nc
    z0_rows = z0.rearrange("(p i) d -> p i d", i=ROW_TILES)
    v0_rows = v0t.rearrange("(p i) d -> p i d", i=ROW_TILES)
    out_rows = out.rearrange("(p i) t h -> p i t h", i=ROW_TILES)

    with ExitStack() as ctx:
        consts = ctx.enter_context(tc.tile_pool(name="consts", bufs=1))
        coef = ctx.enter_context(tc.tile_pool(name="coef", bufs=1))
        unread = ctx.enter_context(tc.tile_pool(name="unread", bufs=4))
        stream = ctx.enter_context(tc.tile_pool(name="stream", bufs=3))
        psum_v0 = ctx.enter_context(tc.psum_pool(name="psum_v0", bufs=2))
        psum_in = ctx.enter_context(tc.psum_pool(name="psum_in", bufs=2))
        psum_mm = ctx.enter_context(tc.psum_pool(name="psum_mm", bufs=2))
        psum_out = ctx.enter_context(tc.psum_pool(name="psum_out", bufs=2))

        z0_sb = consts.tile([P, ROW_TILES, D], BF16)
        v0_sb = consts.tile([P, ROW_TILES, D], BF16)
        raw_step = consts.tile([P, 1], BF16)
        w_raw = consts.tile([P, 4, H], BF16)
        b_rows = consts.tile([P, P], BF16)
        nc.vector.memset(b_rows[:], 0.0)
        nc.sync.dma_start(out=raw_step[:], in_=step_sizes.partition_broadcast(P))
        for first in range(0, ROW_TILES, FIRST_TILES):
            tiles = slice(first, first + FIRST_TILES)
            nc.sync.dma_start(out=z0_sb[:, tiles, :], in_=z0_rows[:, tiles, :])
            nc.sync.dma_start(out=v0_sb[:, tiles, :], in_=v0_rows[:, tiles, :])
            if first == 0:
                for u in range(2):
                    nc.sync.dma_start(
                        out=w_raw[:, 2 * u : 2 * u + 2, :],
                        in_=W1[WORDS * u : WORDS * (u + 1), :].rearrange("(q e) c -> q e c", e=2),
                    )
                nc.sync.dma_start(out=b_rows[0:H_TILES, :], in_=b1.rearrange("(c h) -> c h", c=H_TILES))

        warm = consts.tile([P, 1], F32)
        nc.vector.memset(warm[:], 1.0)
        nc.scalar.activation(out=warm[:], in_=warm[:], func=ACT.Sqrt)

        ident = consts.tile([P, P], F32)
        make_identity(nc, ident[:])
        ident_bf16 = consts.tile([P, P], BF16)
        make_identity(nc, ident_bf16[:])

        step_number = consts.tile([P, STEPS], F32)
        for t in range(STEPS):
            nc.vector.memset(step_number[:, t : t + 1], float(t + 1))

        w_grouped = consts.tile([P, H, 4], BF16, align_bytes=64)
        w_codes = consts.tile([P, H], U32, align_bytes=64)
        w_scales = consts.tile([P, H], U8, align_bytes=64)
        nc.vector.tensor_copy(out=w_grouped[:], in_=w_raw[:].rearrange("p j c -> p c j"))

        b_rows32 = consts.tile([P, P], F32)
        b_col = consts.tile([P, H_TILES], F32)
        nc.vector.tensor_copy(out=b_rows32[:], in_=b_rows[:])
        b_turned = psum_in.tile([P, P], F32, tag="turned")
        nc.tensor.transpose(out=b_turned[:], in_=b_rows32[:], identity=ident[:])
        nc.vector.tensor_copy(out=b_col[:], in_=b_turned[:, 0:H_TILES])
        nc.vector.quantize_mx(
            out=w_codes[:].bitcast(FP8X4), scales=w_scales[:], in_=w_grouped[:].rearrange("p c j -> p (c j)")
        )

        x2 = coef.tile([P, ROW_TILES], F32)
        vv = coef.tile([P, ROW_TILES], F32)
        xv = coef.tile([P, ROW_TILES], F32)

        def scalar_sum_of_squares(x, total):
            squares = unread.tile([P, D], BF16)
            nc.scalar.activation(out=squares[:], in_=x, func=ACT.Square, accum_out=total)

        def vector_sum_of_products(x, y, total):
            products = unread.tile([P, D], F32)
            nc.vector.scalar_tensor_tensor(
                out=products[:], in0=x, scalar=1.0, in1=y, op0=ALU.mult, op1=ALU.mult, accum_out=total
            )

        def row_sums(i):
            z_i, v_i = z0_sb[:, i, :], v0_sb[:, i, :]
            scalar_sum_of_squares(z_i, x2[:, i : i + 1])
            vector_sum_of_products(z_i, v_i, xv[:, i : i + 1])
            if i < ROW_TILES // 2:
                vector_sum_of_products(v_i, v_i, vv[:, i : i + 1])
            else:
                scalar_sum_of_squares(v_i, vv[:, i : i + 1])

        def row_tile(name):
            return coef.tile([P, ROW_TILES], F32, name=name)

        def grid_tile(name):
            return coef.tile([P, ROW_TILES, STEPS], F32, name=name)

        step = consts.tile([P, 1], F32)
        step_t = consts.tile([P, STEPS], F32)
        step_t_capped = consts.tile([P, STEPS], F32)
        one_minus_x2 = row_tile("one_minus_x2")
        half_lambda = row_tile("half_lambda")
        vv_floor = row_tile("vv_floor")
        root_vv = row_tile("root_vv")
        newton_row = row_tile("newton_row")
        inv_root_vv = row_tile("inv_root_vv")
        norm_v = grid_tile("norm_v")
        tanh_arg = grid_tile("tanh_arg")
        tanh_val = grid_tile("tanh_val")
        y_over_v = grid_tile("y_over_v")
        xy = grid_tile("xy")
        y2 = grid_tile("y2")
        two_xy_y2 = grid_tile("two_xy_y2")
        den = grid_tile("den")
        inv_den = grid_tile("inv_den")
        norm2_m = grid_tile("norm2_m")
        norm_m = grid_tile("norm_m")
        newton = grid_tile("newton")
        inv_norm_m = grid_tile("inv_norm_m")
        norm_z = grid_tile("norm_z")
        one_plus = grid_tile("one_plus")
        one_minus = grid_tile("one_minus")
        log_ratio = grid_tile("log_ratio")
        gain = grid_tile("gain")
        gain_z = grid_tile("gain_z")
        gain_v = grid_tile("gain_v")
        alpha = grid_tile("alpha")
        beta = grid_tile("beta")

        def load_table_of(func, after):
            nc.scalar.activation(out=warm[:], in_=after, func=func)

        def step_sizes_times_t():
            nc.scalar.activation(out=step[:], in_=raw_step[:], func=ACT.Tanh, scale=0.5)
            nc.vector.tensor_scalar(out=step[:], in0=step[:], scalar1=0.5, scalar2=0.5, op0=ALU.mult, op1=ALU.add)
            nc.vector.tensor_scalar(out=step_t[:], in0=step_number[:], scalar1=step[:, 0:1], scalar2=None, op0=ALU.mult)
            nc.vector.tensor_scalar(
                out=step_t_capped[:], in0=step_t[:], scalar1=1.0 / math.sqrt(EPS), scalar2=None, op0=ALU.mult
            )

        def coefficients(first, count, with_step):
            shape = [P, count, STEPS]
            v = nc.vector

            def rows(x):
                return x[:, first : first + count]

            def grid(x):
                return x[:, first : first + count, :]

            def over_steps(x):
                return rows(x).unsqueeze(2).to_broadcast(shape)

            def over_rows(x):
                return x[:].unsqueeze(1).to_broadcast(shape)

            v.tensor_scalar(out=rows(one_minus_x2), in0=rows(x2), scalar1=-1.0, scalar2=1.0, op0=ALU.mult, op1=ALU.add)
            v.tensor_scalar_max(out=rows(half_lambda), in0=rows(one_minus_x2), scalar1=EPS)
            v.reciprocal(out=rows(half_lambda), in_=rows(half_lambda))
            v.tensor_scalar_max(out=rows(vv_floor), in0=rows(vv), scalar1=TINY)
            nc.scalar.activation(out=rows(root_vv), in_=rows(vv_floor), func=ACT.Sqrt)
            load_table_of(ACT.Tanh, root_vv[:, first : first + 1])
            v.reciprocal(out=rows(newton_row), in_=rows(root_vv))
            v.scalar_tensor_tensor(
                out=rows(newton_row), in0=rows(vv_floor), scalar=0.5, in1=rows(newton_row), op0=ALU.mult, op1=ALU.mult
            )
            v.scalar_tensor_tensor(
                out=rows(root_vv), in0=rows(root_vv), scalar=0.5, in1=rows(newton_row), op0=ALU.mult, op1=ALU.add
            )
            v.reciprocal(out=rows(inv_root_vv), in_=rows(root_vv))
            if with_step:
                step_sizes_times_t()
            v.tensor_tensor(out=grid(norm_v), in0=over_steps(root_vv), in1=over_rows(step_t), op=ALU.mult)
            v.scalar_tensor_tensor(
                out=grid(tanh_arg), in0=grid(norm_v), scalar=math.sqrt(EPS), in1=over_steps(half_lambda),
                op0=ALU.max, op1=ALU.mult,
            )
            nc.scalar.activation(out=grid(tanh_val), in_=grid(tanh_arg), func=ACT.Tanh)
            load_table_of(ACT.Sqrt, tanh_val[:, first, 0:1])
            v.tensor_tensor(out=grid(y_over_v), in0=over_steps(inv_root_vv), in1=over_rows(step_t_capped), op=ALU.min)
            v.tensor_mul(out=grid(y_over_v), in0=grid(y_over_v), in1=grid(tanh_val))
            v.tensor_tensor(out=grid(xy), in0=grid(y_over_v), in1=over_steps(xv), op=ALU.mult)
            v.tensor_tensor(out=grid(y2), in0=grid(y_over_v), in1=over_steps(vv), op=ALU.mult)
            v.tensor_mul(out=grid(y2), in0=grid(y2), in1=grid(y_over_v))
            v.scalar_tensor_tensor(
                out=grid(two_xy_y2), in0=grid(xy), scalar=2.0, in1=grid(y2), op0=ALU.mult, op1=ALU.add
            )
            v.tensor_tensor(out=grid(den), in0=grid(y2), in1=over_steps(x2), op=ALU.mult)
            v.scalar_tensor_tensor(out=grid(den), in0=grid(xy), scalar=2.0, in1=grid(den), op0=ALU.mult, op1=ALU.add)
            v.tensor_scalar(out=grid(den), in0=grid(den), scalar1=1.0, scalar2=EPS, op0=ALU.add, op1=ALU.max)
            v.reciprocal(out=grid(inv_den), in_=grid(den))
            v.tensor_tensor(out=grid(norm2_m), in0=grid(two_xy_y2), in1=over_steps(x2), op=ALU.add)
            v.tensor_mul(out=grid(norm2_m), in0=grid(norm2_m), in1=grid(inv_den))
            v.tensor_scalar_max(out=grid(norm2_m), in0=grid(norm2_m), scalar1=EPS)
            nc.scalar.activation(out=grid(norm_m), in_=grid(norm2_m), func=ACT.Sqrt)
            load_table_of(ACT.Ln, norm2_m[:, first, 0:1])
            v.reciprocal(out=grid(newton), in_=grid(norm_m))
            v.scalar_tensor_tensor(
                out=grid(newton), in0=grid(norm2_m), scalar=0.5, in1=grid(newton), op0=ALU.mult, op1=ALU.mult
            )
            v.scalar_tensor_tensor(
                out=grid(norm_m), in0=grid(norm_m), scalar=0.5, in1=grid(newton), op0=ALU.mult, op1=ALU.add
            )
            v.tensor_scalar_min(out=grid(norm_z), in0=grid(norm_m), scalar1=MAXN)
            v.tensor_scalar(out=grid(one_minus), in0=grid(norm_z), scalar1=-1.0, scalar2=1.0, op0=ALU.mult, op1=ALU.add)
            v.reciprocal(out=grid(one_minus), in_=grid(one_minus))
            v.tensor_scalar_add(out=grid(one_plus), in0=grid(norm_z), scalar1=1.0)
            v.tensor_mul(out=grid(one_plus), in0=grid(one_plus), in1=grid(one_minus))
            nc.scalar.activation(out=grid(log_ratio), in_=grid(one_plus), func=ACT.Ln)
            load_table_of(ACT.Sqrt, one_plus[:, first, 0:1])
            v.reciprocal(out=grid(inv_norm_m), in_=grid(norm_m))
            v.tensor_mul(out=grid(gain), in0=grid(inv_norm_m), in1=grid(inv_den))
            v.scalar_tensor_tensor(
                out=grid(gain_z), in0=grid(two_xy_y2), scalar=1.0, in1=grid(gain), op0=ALU.add, op1=ALU.mult
            )
            v.tensor_mul(out=grid(gain_v), in0=grid(y_over_v), in1=grid(gain))
            v.tensor_tensor(out=grid(gain_v), in0=grid(gain_v), in1=over_steps(one_minus_x2), op=ALU.mult)
            v.scalar_tensor_tensor(
                out=grid(alpha), in0=grid(log_ratio), scalar=0.5, in1=grid(gain_z), op0=ALU.mult, op1=ALU.mult
            )
            v.scalar_tensor_tensor(
                out=grid(beta), in0=grid(log_ratio), scalar=0.5, in1=grid(gain_v), op0=ALU.mult, op1=ALU.mult
            )

        for i in range(FIRST_TILES):
            row_sums(i)
        coefficients(0, FIRST_TILES, True)
        for i in range(FIRST_TILES, ROW_TILES):
            row_sums(i)
        coefficients(FIRST_TILES, ROW_TILES - FIRST_TILES, False)

        scaled_z, v0_psum, tan, turned, grouped, codes, scales = {}, {}, {}, {}, {}, {}, {}
        acc, hidden, back, result = {}, {}, {}, {}

        def scale(s):
            i = s // 2
            scaled_z[s] = []
            for q in range(HALF):
                t = (s % 2) * HALF + q
                scaled = stream.tile([P, D], F32, bufs=2 * HALF)
                nc.gpsimd.tensor_scalar(
                    out=scaled[:], in0=z0_sb[:, i, :], scalar1=alpha[:, i, t : t + 1], scalar2=0.0,
                    op0=ALU.mult, op1=ALU.add,
                )
                scaled_z[s].append(scaled)

        def copy_v0(i):
            v0_psum[i] = psum_v0.tile([P, D], F32, name="v0_copy")
            nc.tensor.matmul(out=v0_psum[i][:], lhsT=ident_bf16[:], rhs=v0_sb[:, i, :], start=True, stop=True)

        def combine(s):
            i = s // 2
            tan[s] = stream.tile([P, HALF * D], BF16, name="tan")
            for q in range(HALF):
                t = (s % 2) * HALF + q
                nc.vector.scalar_tensor_tensor(
                    out=tan[s][:, q * D : (q + 1) * D], in0=v0_psum[i][:], scalar=beta[:, i, t : t + 1],
                    in1=scaled_z[s][q][:], op0=ALU.mult, op1=ALU.add,
                )

        def turn_in(m):
            s, pair = divmod(m, 2)
            tan_words = tan[s][:].bitcast(F32)
            turned[m] = psum_in.tile([P, 2, 2 * P], F32, name="turned", tag="turned")
            for q in range(2):
                for u in range(2):
                    first_word = (2 * pair + q) * WORDS + u * P
                    nc.tensor.transpose(
                        out=turned[m][:, u, q * P : (q + 1) * P],
                        in_=tan_words[:, first_word : first_word + P],
                        identity=ident[:],
                    )

        def gather(m):
            s, pair = divmod(m, 2)
            if pair == 0:
                grouped[s] = stream.tile([P, HALF * P * 4], BF16, name="grouped", align_bytes=64)
            grouped_words = grouped[s][:].bitcast(F32).rearrange("p (c u) -> p c u", u=2)
            nc.scalar.copy(
                out=grouped_words[:, pair * 2 * P : (pair + 1) * 2 * P, :],
                in_=turned[m][:].rearrange("p u c -> p c u"),
            )

        def quantise(s):
            codes[s] = stream.tile([P, HALF * P], U32, name="codes", align_bytes=64)
            scales[s] = stream.tile([P, HALF * P], U8, name="scales", align_bytes=64)
            nc.vector.quantize_mx(out=codes[s][:].bitcast(FP8X4), scales=scales[s][:], in_=grouped[s][:])

        def multiply(m):
            s, c = divmod(m, 2)
            units = slice(c * P, (c + 1) * P)
            acc[m] = psum_mm.tile([P, HALF * P], F32, name="acc")
            for repeat in range(MX_REPEATS):
                nc.tensor.matmul_mx(
                    out=acc[m][:],
                    lhsT=w_codes[:, units].bitcast(FP8X4),
                    lhsT_scale=w_scales[:, units],
                    rhs=codes[s][:].bitcast(FP8X4),
                    rhs_scale=scales[s][:],
                    start=True,
                    stop=True,
                )

        def activate(m):
            c = m % 2
            hidden[m] = stream.tile([P, HALF * P], F32, name="hidden")
            nc.scalar.activation(out=hidden[m][:], in_=acc[m][:], func=ACT.Relu, bias=b_col[:, c : c + 1], scale=1.0)

        def turn_out(m):
            back[m] = psum_out.tile([P, HALF, P], F32, name="back")
            for q in range(HALF):
                nc.tensor.transpose(out=back[m][:, q, :], in_=hidden[m][:, q * P : (q + 1) * P], identity=ident[:])

        def collect(m):
            s, c = divmod(m, 2)
            units = slice(c * P, (c + 1) * P)
            if c == 0:
                result[s] = stream.tile([P, HALF, H], F32, name="result")
            if m % 4 == 3:
                nc.vector.tensor_copy(out=result[s][:, :, units], in_=back[m][:])
            else:
                nc.scalar.copy(out=result[s][:, :, units], in_=back[m][:])
            if c == 1:
                first_step = (s % 2) * HALF
                nc.sync.dma_start(out=out_rows[:, s // 2, first_step : first_step + HALF, :], in_=result[s][:])

        def if_any(stage, index, count):
            if 0 <= index < count:
                stage(index)

        with tc.manual_schedule():
            for m in range(-10, BANKS + 1):
                if m % 2 == 0:
                    n = m // 2
                    if_any(scale, n + 5, HALVES)
                    if (n + 5) % 2 == 0:
                        if_any(copy_v0, (n + 5) // 2, ROW_TILES)
                    if_any(quantise, n + 1, HALVES)
                    if_any(combine, n + 4, HALVES)
                if_any(turn_out, m - 1, BANKS)
                if_any(turn_in, m + 5, BANKS)
                if_any(multiply, m + 1, BANKS)
                if_any(activate, m, BANKS)
                if_any(gather, m + 4, BANKS)
                if_any(collect, m - 1, BANKS)
